import numpy as np
import ml_dtypes


def mxq(x, axis, fmt="e4m3"):
    dtype, down = {"e4m3": (ml_dtypes.float8_e4m3fn, 7), "e5m2": (ml_dtypes.float8_e5m2, 14)}[fmt]
    v = np.moveaxis(np.asarray(x, np.float32).astype(ml_dtypes.bfloat16).astype(np.float64), axis, -1)
    blocks = v.reshape(v.shape[:-1] + (-1, 32))
    amax = np.abs(blocks).max(-1, keepdims=True)
    byte = np.maximum(np.where(amax > 0, np.frexp(amax)[1] - 1 + 127, 0) - down, 1)
    scale = np.exp2(byte - 127.0)
    codes = (blocks / scale).astype(np.float32).astype(dtype).astype(np.float64)
    return np.moveaxis((codes * scale).reshape(v.shape), -1, axis)


WIDE = False


def mx_kscale(k):
    if not WIDE:
        return np.ones(k)
    levels = np.array([20, -20, 10, -10, 0])
    a = np.random.permutation(np.resize(levels, k // 512 * 4)).reshape(k // 512, 4)
    idx = np.arange(k)
    return np.exp2(a[idx // 512, idx % 128 // 32])


BF16 = ml_dtypes.bfloat16


def bf(x):
    return np.asarray(x, np.float32).astype(BF16)


def f64(x):
    return np.asarray(x).astype(np.float64)


B, T, M, K, N, IN_MATS, OUT_MATS = 4, 512, 4, 16, 32, 32, 16
KO = OUT_MATS * N
WID = IN_MATS * K
KC = IN_MATS * K
IN_FEATURES = IN_MATS * M * K
OUT_FEATURES = OUT_MATS * M * N


def setup_inputs():
    u = mx_kscale(KO).reshape(OUT_MATS, N)
    x = np.random.standard_normal((B, T, IN_MATS, M, K))
    weight = np.random.standard_normal((OUT_MATS, IN_MATS, N, K)) / np.sqrt(KC) / u[:, None, :, None]
    bias = np.random.standard_normal((OUT_MATS, M, N)) * 0.3
    g = np.random.standard_normal((B, T, OUT_MATS, M, N)) * np.exp2(np.random.randint(-12, 1, (B, T, 1, 1, 1))) * 8.0 * u[:, None, :]
    return {"x": bf(x.reshape(B, T, IN_FEATURES)), "weight": bf(weight), "bias": bf(bias),
            "grad_out": bf(g.reshape(B, T, OUT_FEATURES))}


def reference(x, weight, bias, grad_out):
    Bc, Tc, _ = grad_out.shape
    gb = f64(grad_out).reshape(Bc, Tc, OUT_MATS, M, N)
    gr = gb.transpose(0, 1, 3, 2, 4).reshape(Bc, Tc, M, KO)
    wr = f64(weight).transpose(1, 3, 0, 2).reshape(WID, KO)
    res = mxq(gr, 3, "e5m2") @ mxq(wr, 1, "e4m3").T
    res = res.reshape(Bc, Tc, M, IN_MATS, K).transpose(0, 1, 3, 2, 4)
    return res.reshape(Bc, Tc, IN_FEATURES)

@@ -1,0 +1,137 @@
+import concourse.mybir as mybir
+from concourse.masks import make_identity
+
+FLOPS = 2 * 8192 * 512 * 512
+BYTES = 2048 * 2048 * 2 + 512 * 512 * 2 + 2048 * 2048 * 4
+
+BF16 = mybir.dt.bfloat16
+F32 = mybir.dt.float32
+U32 = mybir.dt.uint32
+U8 = mybir.dt.uint8
+E4 = mybir.dt.float8_e4m3fn_x4
+E5 = mybir.dt.float8_e5m2_x4
+
+P = 128
+NT = 16
+FEAT = 2048
+LOAD_CHUNKS = [1, 1, 2, 4, 4, 4]
+STORE_TILES = 2
+
+
+def tile_blocklinear_t_kernel(tc, x, weight, bias, grad_out, out):
+    nc = tc.nc
+    gv = grad_out.flatten_outer_dims().rearrange("(p i) f -> p i f", i=NT)
+    ov = out.flatten_outer_dims().rearrange("(p i) f -> p i f", i=NT)
+
+    with tc.tile_pool(name="const", bufs=1) as const, tc.tile_pool(name="gin", bufs=1) as gin, tc.tile_pool(
+        name="work", bufs=3
+    ) as work, tc.tile_pool(name="quant", bufs=6) as quant, tc.tile_pool(name="outp", bufs=4) as outp, tc.psum_pool(
+        name="pst", bufs=4
+    ) as pst, tc.psum_pool(name="pso", bufs=4) as pso:
+        w0 = const.tile([P, 4, 512], BF16, name="w0")
+        nc.sync.dma_start(out=w0[:], in_=weight.rearrange("(oh ol) c n k -> (ol c) oh (n k)", ol=4))
+        g_of = []
+        i0 = 0
+        for ci, r in enumerate(LOAD_CHUNKS):
+            gt = gin.tile([P, r, FEAT], BF16, name="g%d" % ci)
+            nc.sync.dma_start(out=gt[:], in_=gv[:, i0 : i0 + r, :])
+            for j in range(r):
+                g_of.append((gt, j))
+            i0 += r
+
+        ident = const.tile([P, P], F32, name="ident")
+        make_identity(nc, ident[:])
+
+        s1 = const.tile([P, FEAT], BF16, name="s1", align_bytes=64)
+        src1 = w0[:].rearrange("p oh (u q ek) -> p u ek oh q", u=2, q=8, ek=32)
+        dst1 = s1[:].rearrange("p (u ek oh q) -> p u ek oh q", u=2, ek=32, oh=4, q=8)
+        nc.vector.tensor_copy(out=dst1[:, 0], in_=src1[:, 0])
+        nc.scalar.copy(out=dst1[:, 1], in_=src1[:, 1])
+        d1 = const.tile([P, FEAT], BF16, name="d1", align_bytes=64)
+        for h in range(2):
+            nc.vector.transpose(out=d1[:, h * 1024 : (h + 1) * 1024], in_=s1[:, h * 1024 : (h + 1) * 1024])
+        wg = const.tile([P, FEAT], BF16, name="wg", align_bytes=64)
+        src2 = d1[:].rearrange("p (t k c) -> p c k t", t=4, k=16, c=32)
+        dst2 = wg[:].rearrange("p (c k t) -> p c k t", c=32, k=16, t=4)
+        nc.vector.tensor_copy(out=dst2[:, 0:16], in_=src2[:, 0:16])
+        nc.scalar.copy(out=dst2[:, 16:32], in_=src2[:, 16:32])
+        wcodes = const.tile([P, 512], U32, name="wcodes", align_bytes=64)
+        wsc = const.tile([P, 512], U8, name="wsc", align_bytes=64)
+        nc.vector.quantize_mx(out=wcodes[:].bitcast(E4), scales=wsc[:], in_=wg[:])
+
+        g2s = {}
+        xts = {}
+        grs = {}
+        cds = {}
+        osb = {}
+
+        def regroup(i):
+            gt, j = g_of[i]
+            g2 = work.tile([P, FEAT], BF16, name="g2", tag="g2", align_bytes=64)
+            nc.vector.tensor_copy(
+                out=g2[:].rearrange("p (mu ol oh x) -> p mu ol oh x", mu=8, ol=4, oh=4, x=16),
+                in_=gt[:, j, :].rearrange("p (oh ol mu x) -> p mu ol oh x", oh=4, ol=4, mu=8, x=16),
+            )
+            g2s[i] = g2
+
+        def transposes(i):
+            g2w = g2s[i][:].bitcast(F32)
+            banks = []
+            for b in range(2):
+                xt = pst.tile([P, 4, P], F32, name="xt", tag="xt")
+                for mu in range(4):
+                    col = (b * 4 + mu) * P
+                    nc.tensor.transpose(xt[:, mu, :], g2w[:, col : col + P], ident[:])
+                banks.append(xt)
+            xts[i] = banks
+
+        def copy_out(i):
+            gr = work.tile([P, FEAT], BF16, name="gr", tag="gr", align_bytes=64)
+            grw = gr[:].bitcast(F32)
+            for b in range(2):
+                nc.vector.tensor_copy(
+                    out=grw[:, b * 512 : (b + 1) * 512].rearrange("p (m t u) -> p m t u", m=2, t=P, u=2),
+                    in_=xts[i][b][:].rearrange("p (m u) t -> p m t u", m=2, u=2),
+                )
+            grs[i] = gr
+
+        def quantise(i):
+            cd = quant.tile([P, 512], U32, name="cd", tag="cd", align_bytes=64)
+            sc = quant.tile([P, 512], U8, name="sc", tag="sc", align_bytes=64)
+            nc.vector.quantize_mx(out=cd[:].bitcast(E5), scales=sc[:], in_=grs[i][:])
+            cds[i] = (cd, sc)
+
+        def multiply(i):
+            cd, sc = cds[i]
+            j = i % STORE_TILES
+            if j == 0:
+                ot = outp.tile([P, STORE_TILES, FEAT], F32, name="ot", tag="ot")
+                osb[i // STORE_TILES] = ot
+            ot = osb[i // STORE_TILES]
+            oview = ot[:, j, :].rearrange("p (c m k) -> p c m k", c=32, m=4, k=16)
+            for m in range(4):
+                acc = pso.tile([P, 512], F32, name="acc", tag="acc")
+                nc.tensor.matmul_mx(
+                    out=acc[:],
+                    lhsT=cd[:, m * P : (m + 1) * P].bitcast(E5),
+                    lhsT_scale=sc[:, m * P : (m + 1) * P],
+                    rhs=wcodes[:].bitcast(E4),
+                    rhs_scale=wsc[:],
+                    start=True,
+                    stop=True,
+                )
+                nc.scalar.copy(out=oview[:, :, m, :], in_=acc[:].rearrange("p (c k) -> p c k", c=32))
+            if j == STORE_TILES - 1:
+                nc.sync.dma_start(out=ov[:, i - j : i + 1, :], in_=ot[:])
+
+        for s in range(NT + 4):
+            if s < NT:
+                regroup(s)
+            if 0 <= s - 1 < NT:
+                transposes(s - 1)
+            if 0 <= s - 2 < NT:
+                copy_out(s - 2)
+            if 0 <= s - 3 < NT:
+                quantise(s - 3)
+            if 0 <= s - 4 < NT:
+                multiply(s - 4)

@@ -15,7 +15,9 @@ P = 128
 NT = 16
 FEAT = 2048
 LOAD_CHUNKS = [1, 1, 2, 4, 4, 4]
-STORE_TILES = 2
+STORE_CHUNKS = [2, 2, 2, 2, 2, 2, 2, 1, 1]
+HEAD_TILES = 4
+TAIL_FROM = 8
 
 
 def tile_blocklinear_t_kernel(tc, x, weight, bias, grad_out, out):
@@ -43,21 +45,33 @@ def tile_blocklinear_t_kernel(tc, x, weight, bias, grad_out, out):
         make_identity(nc, ident[:])
 
         s1 = const.tile([P, FEAT], BF16, name="s1", align_bytes=64)
-        src1 = w0[:].rearrange("p oh (u q ek) -> p u ek oh q", u=2, q=8, ek=32)
-        dst1 = s1[:].rearrange("p (u ek oh q) -> p u ek oh q", u=2, ek=32, oh=4, q=8)
-        nc.vector.tensor_copy(out=dst1[:, 0], in_=src1[:, 0])
-        nc.scalar.copy(out=dst1[:, 1], in_=src1[:, 1])
         d1 = const.tile([P, FEAT], BF16, name="d1", align_bytes=64)
-        for h in range(2):
-            nc.vector.transpose(out=d1[:, h * 1024 : (h + 1) * 1024], in_=s1[:, h * 1024 : (h + 1) * 1024])
         wg = const.tile([P, FEAT], BF16, name="wg", align_bytes=64)
-        src2 = d1[:].rearrange("p (t k c) -> p c k t", t=4, k=16, c=32)
-        dst2 = wg[:].rearrange("p (c k t) -> p c k t", c=32, k=16, t=4)
-        nc.vector.tensor_copy(out=dst2[:, 0:16], in_=src2[:, 0:16])
-        nc.scalar.copy(out=dst2[:, 16:32], in_=src2[:, 16:32])
         wcodes = const.tile([P, 512], U32, name="wcodes", align_bytes=64)
         wsc = const.tile([P, 512], U8, name="wsc", align_bytes=64)
-        nc.vector.quantize_mx(out=wcodes[:].bitcast(E4), scales=wsc[:], in_=wg[:])
+
+        def weight_stage(s):
+            if s == 0:
+                src1 = w0[:].rearrange("p oh (u q ek) -> p u ek oh q", u=2, q=8, ek=32)
+                dst1 = s1[:].rearrange("p (u ek oh q) -> p u ek oh q", u=2, ek=32, oh=4, q=8)
+                nc.vector.tensor_copy(out=dst1[:, 0], in_=src1[:, 0])
+                nc.scalar.copy(out=dst1[:, 1], in_=src1[:, 1])
+            elif s <= 2:
+                h = s - 1
+                nc.vector.transpose(out=d1[:, h * 1024 : (h + 1) * 1024], in_=s1[:, h * 1024 : (h + 1) * 1024])
+            elif s == 3:
+                src2 = d1[:].rearrange("p (t k c) -> p c k t", t=4, k=16, c=32)
+                dst2 = wg[:].rearrange("p (c k t) -> p c k t", c=32, k=16, t=4)
+                nc.vector.tensor_copy(out=dst2[:, 0:16], in_=src2[:, 0:16])
+                nc.scalar.copy(out=dst2[:, 16:32], in_=src2[:, 16:32])
+                nc.vector.quantize_mx(out=wcodes[:].bitcast(E4), scales=wsc[:], in_=wg[:])
+
+        store_of = []
+        first = 0
+        for r in STORE_CHUNKS:
+            for j in range(r):
+                store_of.append((first, r))
+            first += r
 
         g2s = {}
         xts = {}
@@ -89,10 +103,12 @@ def tile_blocklinear_t_kernel(tc, x, weight, bias, grad_out, out):
             gr = work.tile([P, FEAT], BF16, name="gr", tag="gr", align_bytes=64)
             grw = gr[:].bitcast(F32)
             for b in range(2):
-                nc.vector.tensor_copy(
-                    out=grw[:, b * 512 : (b + 1) * 512].rearrange("p (m t u) -> p m t u", m=2, t=P, u=2),
-                    in_=xts[i][b][:].rearrange("p (m u) t -> p m t u", m=2, u=2),
-                )
+                dst = grw[:, b * 512 : (b + 1) * 512].rearrange("p (m t u) -> p m t u", m=2, t=P, u=2)
+                src = xts[i][b][:].rearrange("p (m u) t -> p m t u", m=2, u=2)
+                if i < HEAD_TILES:
+                    nc.scalar.copy(out=dst, in_=src)
+                else:
+                    nc.vector.tensor_copy(out=dst, in_=src)
             grs[i] = gr
 
         def quantise(i):
@@ -103,11 +119,11 @@ def tile_blocklinear_t_kernel(tc, x, weight, bias, grad_out, out):
 
         def multiply(i):
             cd, sc = cds[i]
-            j = i % STORE_TILES
+            first, r = store_of[i]
+            j = i - first
             if j == 0:
-                ot = outp.tile([P, STORE_TILES, FEAT], F32, name="ot", tag="ot")
-                osb[i // STORE_TILES] = ot
-            ot = osb[i // STORE_TILES]
+                osb[first] = outp.tile([P, r, FEAT], F32, name="ot", tag="ot")
+            ot = osb[first]
             oview = ot[:, j, :].rearrange("p (c m k) -> p c m k", c=32, m=4, k=16)
             for m in range(4):
                 acc = pso.tile([P, 512], F32, name="acc", tag="acc")
@@ -120,18 +136,23 @@ def tile_blocklinear_t_kernel(tc, x, weight, bias, grad_out, out):
                     start=True,
                     stop=True,
                 )
-                nc.scalar.copy(out=oview[:, :, m, :], in_=acc[:].rearrange("p (c k) -> p c k", c=32))
-            if j == STORE_TILES - 1:
-                nc.sync.dma_start(out=ov[:, i - j : i + 1, :], in_=ot[:])
+                if m == 3 and i >= TAIL_FROM:
+                    nc.vector.tensor_copy(out=oview[:, :, m, :], in_=acc[:].rearrange("p (c k) -> p c k", c=32))
+                else:
+                    nc.scalar.copy(out=oview[:, :, m, :], in_=acc[:].rearrange("p (c k) -> p c k", c=32))
+            if j == r - 1:
+                nc.sync.dma_start(out=ov[:, first : first + r, :], in_=ot[:])
 
-        for s in range(NT + 4):
-            if s < NT:
-                regroup(s)
-            if 0 <= s - 1 < NT:
-                transposes(s - 1)
-            if 0 <= s - 2 < NT:
-                copy_out(s - 2)
-            if 0 <= s - 3 < NT:
-                quantise(s - 3)
-            if 0 <= s - 4 < NT:
-                multiply(s - 4)
+        with tc.manual_schedule():
+            for s in range(NT + 4):
+                weight_stage(s)
+                if s < NT:
+                    regroup(s)
+                if 0 <= s - 3 < NT:
+                    quantise(s - 3)
+                if 0 <= s - 1 < NT:
+                    transposes(s - 1)
+                if 0 <= s - 2 < NT:
+                    copy_out(s - 2)
+                if 0 <= s - 4 < NT:
+                    multiply(s - 4)

@@ -16,8 +16,8 @@ NT = 16
 FEAT = 2048
 LOAD_CHUNKS = [1, 1, 2, 4, 4, 4]
 STORE_CHUNKS = [2, 2, 2, 2, 2, 2, 2, 1, 1]
-HEAD_TILES = 4
-TAIL_FROM = 8
+HEAD_TILES = 2
+TAIL_TILES = 2
 
 
 def tile_blocklinear_t_kernel(tc, x, weight, bias, grad_out, out):
@@ -44,27 +44,29 @@ def tile_blocklinear_t_kernel(tc, x, weight, bias, grad_out, out):
         ident = const.tile([P, P], F32, name="ident")
         make_identity(nc, ident[:])
 
-        s1 = const.tile([P, FEAT], BF16, name="s1", align_bytes=64)
-        d1 = const.tile([P, FEAT], BF16, name="d1", align_bytes=64)
+        s1 = const.tile([P, 1024], F32, name="s1", align_bytes=64)
+        d1 = const.tile([P, 1024], F32, name="d1", align_bytes=64)
         wg = const.tile([P, FEAT], BF16, name="wg", align_bytes=64)
         wcodes = const.tile([P, 512], U32, name="wcodes", align_bytes=64)
         wsc = const.tile([P, 512], U8, name="wsc", align_bytes=64)
 
-        def weight_stage(s):
-            if s == 0:
-                src1 = w0[:].rearrange("p oh (u q ek) -> p u ek oh q", u=2, q=8, ek=32)
-                dst1 = s1[:].rearrange("p (u ek oh q) -> p u ek oh q", u=2, ek=32, oh=4, q=8)
-                nc.vector.tensor_copy(out=dst1[:, 0], in_=src1[:, 0])
-                nc.scalar.copy(out=dst1[:, 1], in_=src1[:, 1])
-            elif s <= 2:
-                h = s - 1
-                nc.vector.transpose(out=d1[:, h * 1024 : (h + 1) * 1024], in_=s1[:, h * 1024 : (h + 1) * 1024])
-            elif s == 3:
-                src2 = d1[:].rearrange("p (t k c) -> p c k t", t=4, k=16, c=32)
-                dst2 = wg[:].rearrange("p (c k t) -> p c k t", c=32, k=16, t=4)
-                nc.vector.tensor_copy(out=dst2[:, 0:16], in_=src2[:, 0:16])
-                nc.scalar.copy(out=dst2[:, 16:32], in_=src2[:, 16:32])
-                nc.vector.quantize_mx(out=wcodes[:].bitcast(E4), scales=wsc[:], in_=wg[:])
+        def weight_permute():
+            src1 = w0[:].bitcast(F32).rearrange("p oh (u q f) -> p u f oh q", u=2, q=8, f=16)
+            dst1 = s1[:].rearrange("p (u f oh q) -> p u f oh q", u=2, f=16, oh=4, q=8)
+            nc.vector.tensor_copy(out=dst1[:, 0], in_=src1[:, 0])
+            nc.scalar.copy(out=dst1[:, 1], in_=src1[:, 1])
+
+        def weight_transpose(h):
+            nc.vector.transpose(out=d1[:, h * 512 : (h + 1) * 512], in_=s1[:, h * 512 : (h + 1) * 512])
+
+        def weight_interleave():
+            nc.vector.tensor_copy(
+                out=wg[:].rearrange("p (c k2 kp t) -> p c k2 kp t", c=32, k2=8, kp=2, t=4),
+                in_=d1[:].bitcast(BF16).rearrange("p (t k2 c kp) -> p c k2 kp t", t=4, k2=8, c=32, kp=2),
+            )
+
+        def weight_quantise():
+            nc.vector.quantize_mx(out=wcodes[:].bitcast(E4), scales=wsc[:], in_=wg[:])
 
         store_of = []
         first = 0
@@ -136,7 +138,7 @@ def tile_blocklinear_t_kernel(tc, x, weight, bias, grad_out, out):
                     start=True,
                     stop=True,
                 )
-                if m == 3 and i >= TAIL_FROM:
+                if m >= 2 and i >= NT - TAIL_TILES:
                     nc.vector.tensor_copy(out=oview[:, :, m, :], in_=acc[:].rearrange("p (c k) -> p c k", c=32))
                 else:
                     nc.scalar.copy(out=oview[:, :, m, :], in_=acc[:].rearrange("p (c k) -> p c k", c=32))
@@ -144,15 +146,27 @@ def tile_blocklinear_t_kernel(tc, x, weight, bias, grad_out, out):
                 nc.sync.dma_start(out=ov[:, first : first + r, :], in_=ot[:])
 
         with tc.manual_schedule():
-            for s in range(NT + 4):
-                weight_stage(s)
-                if s < NT:
-                    regroup(s)
-                if 0 <= s - 3 < NT:
-                    quantise(s - 3)
-                if 0 <= s - 1 < NT:
-                    transposes(s - 1)
-                if 0 <= s - 2 < NT:
-                    copy_out(s - 2)
-                if 0 <= s - 4 < NT:
-                    multiply(s - 4)
+            weight_permute()
+            regroup(0)
+            weight_transpose(0)
+            transposes(0)
+            weight_transpose(1)
+            regroup(1)
+            copy_out(0)
+            transposes(1)
+            weight_interleave()
+            copy_out(1)
+            weight_quantise()
+            quantise(0)
+            quantise(1)
+            regroup(2)
+            for i in range(NT):
+                if 2 <= i + 1 < NT:
+                    copy_out(i + 1)
+                if i + 3 < NT:
+                    regroup(i + 3)
+                if 2 <= i + 1 < NT:
+                    quantise(i + 1)
+                multiply(i)
+                if i + 2 < NT:
+                    transposes(i + 2)

@@ -16,6 +16,7 @@ NT = 16
 FEAT = 2048
 LOAD_CHUNKS = [1, 1, 2, 4, 4, 4]
 STORE_CHUNKS = [2, 2, 2, 2, 2, 2, 2, 1, 1]
+SCALAR_QUEUE_CHUNKS = (3, 5)
 HEAD_TILES = 2
 TAIL_TILES = 2
 
@@ -33,10 +34,14 @@ def tile_blocklinear_t_kernel(tc, x, weight, bias, grad_out, out):
         w0 = const.tile([P, 4, 512], BF16, name="w0")
         nc.sync.dma_start(out=w0[:], in_=weight.rearrange("(oh ol) c n k -> (ol c) oh (n k)", ol=4))
         g_of = []
+        late_loads = []
         i0 = 0
         for ci, r in enumerate(LOAD_CHUNKS):
             gt = gin.tile([P, r, FEAT], BF16, name="g%d" % ci)
-            nc.sync.dma_start(out=gt[:], in_=gv[:, i0 : i0 + r, :])
+            if ci in SCALAR_QUEUE_CHUNKS:
+                late_loads.append((gt, i0, r))
+            else:
+                nc.sync.dma_start(out=gt[:], in_=gv[:, i0 : i0 + r, :])
             for j in range(r):
                 g_of.append((gt, j))
             i0 += r
@@ -147,6 +152,8 @@ def tile_blocklinear_t_kernel(tc, x, weight, bias, grad_out, out):
 
         with tc.manual_schedule():
             weight_permute()
+            for gt, i0, r in late_loads:
+                nc.scalar.dma_start(out=gt[:], in_=gv[:, i0 : i0 + r, :])
             regroup(0)
             weight_transpose(0)
             transposes(0)

@@ -31,13 +31,13 @@ def tile_blocklinear_t_kernel(tc, x, weight, bias, grad_out, out):
     ) as work, tc.tile_pool(name="quant", bufs=6) as quant, tc.tile_pool(name="outp", bufs=4) as outp, tc.psum_pool(
         name="pst", bufs=4
     ) as pst, tc.psum_pool(name="pso", bufs=4) as pso:
-        w0 = const.tile([P, 4, 512], BF16, name="w0")
+        w0 = const.tile([P, 4, 512], BF16, name="w0", align_bytes=256)
         nc.sync.dma_start(out=w0[:], in_=weight.rearrange("(oh ol) c n k -> (ol c) oh (n k)", ol=4))
         g_of = []
         late_loads = []
         i0 = 0
         for ci, r in enumerate(LOAD_CHUNKS):
-            gt = gin.tile([P, r, FEAT], BF16, name="g%d" % ci)
+            gt = gin.tile([P, r, FEAT], BF16, name="g%d" % ci, align_bytes=256)
             if ci in SCALAR_QUEUE_CHUNKS:
                 late_loads.append((gt, i0, r))
             else:
@@ -129,7 +129,7 @@ def tile_blocklinear_t_kernel(tc, x, weight, bias, grad_out, out):
             first, r = store_of[i]
             j = i - first
             if j == 0:
-                osb[first] = outp.tile([P, r, FEAT], F32, name="ot", tag="ot")
+                osb[first] = outp.tile([P, r, FEAT], F32, name="ot", tag="ot", align_bytes=256)
             ot = osb[first]
             oview = ot[:, j, :].rearrange("p (c m k) -> p c m k", c=32, m=4, k=16)
             for m in range(4):

import concourse.mybir as mybir
from concourse.masks import make_identity

FLOPS = 2 * 8192 * 512 * 512
BYTES = 2048 * 2048 * 2 + 512 * 512 * 2 + 2048 * 2048 * 4

BF16 = mybir.dt.bfloat16
F32 = mybir.dt.float32
U32 = mybir.dt.uint32
U8 = mybir.dt.uint8
E4 = mybir.dt.float8_e4m3fn_x4
E5 = mybir.dt.float8_e5m2_x4

P = 128
NT = 16
FEAT = 2048
LOAD_CHUNKS = [1, 1, 2, 4, 4, 4]
STORE_CHUNKS = [2, 2, 2, 2, 2, 2, 2, 1, 1]
SCALAR_QUEUE_CHUNKS = (3, 5)
HEAD_TILES = 2
TAIL_TILES = 2


def tile_blocklinear_t_kernel(tc, x, weight, bias, grad_out, out):
    nc = tc.nc
    gv = grad_out.flatten_outer_dims().rearrange("(p i) f -> p i f", i=NT)
    ov = out.flatten_outer_dims().rearrange("(p i) f -> p i f", i=NT)

    with tc.tile_pool(name="const", bufs=1) as const, tc.tile_pool(name="gin", bufs=1) as gin, tc.tile_pool(
        name="work", bufs=3
    ) as work, tc.tile_pool(name="quant", bufs=6) as quant, tc.tile_pool(name="outp", bufs=4) as outp, tc.psum_pool(
        name="pst", bufs=4
    ) as pst, tc.psum_pool(name="pso", bufs=4) as pso:
        w0 = const.tile([P, 4, 512], BF16, name="w0", align_bytes=256)
        nc.sync.dma_start(out=w0[:], in_=weight.rearrange("(oh ol) c n k -> (ol c) oh (n k)", ol=4))
        g_of = []
        late_loads = []
        i0 = 0
        for ci, r in enumerate(LOAD_CHUNKS):
            gt = gin.tile([P, r, FEAT], BF16, name="g%d" % ci, align_bytes=256)
            if ci in SCALAR_QUEUE_CHUNKS:
                late_loads.append((gt, i0, r))
            else:
                nc.sync.dma_start(out=gt[:], in_=gv[:, i0 : i0 + r, :])
            for j in range(r):
                g_of.append((gt, j))
            i0 += r

        ident = const.tile([P, P], F32, name="ident")
        make_identity(nc, ident[:])

        s1 = const.tile([P, 1024], F32, name="s1", align_bytes=64)
        d1 = const.tile([P, 1024], F32, name="d1", align_bytes=64)
        wg = const.tile([P, FEAT], BF16, name="wg", align_bytes=64)
        wcodes = const.tile([P, 512], U32, name="wcodes", align_bytes=64)
        wsc = const.tile([P, 512], U8, name="wsc", align_bytes=64)

        def weight_permute():
            src1 = w0[:].bitcast(F32).rearrange("p oh (u q f) -> p u f oh q", u=2, q=8, f=16)
            dst1 = s1[:].rearrange("p (u f oh q) -> p u f oh q", u=2, f=16, oh=4, q=8)
            nc.vector.tensor_copy(out=dst1[:, 0], in_=src1[:, 0])
            nc.scalar.copy(out=dst1[:, 1], in_=src1[:, 1])

        def weight_transpose(h):
            nc.vector.transpose(out=d1[:, h * 512 : (h + 1) * 512], in_=s1[:, h * 512 : (h + 1) * 512])

        def weight_interleave():
            nc.vector.tensor_copy(
                out=wg[:].rearrange("p (c k2 kp t) -> p c k2 kp t", c=32, k2=8, kp=2, t=4),
                in_=d1[:].bitcast(BF16).rearrange("p (t k2 c kp) -> p c k2 kp t", t=4, k2=8, c=32, kp=2),
            )

        def weight_quantise():
            nc.vector.quantize_mx(out=wcodes[:].bitcast(E4), scales=wsc[:], in_=wg[:])

        store_of = []
        first = 0
        for r in STORE_CHUNKS:
            for j in range(r):
                store_of.append((first, r))
            first += r

        g2s = {}
        xts = {}
        grs = {}
        cds = {}
        osb = {}

        def regroup(i):
            gt, j = g_of[i]
            g2 = work.tile([P, FEAT], BF16, name="g2", tag="g2", align_bytes=64)
            nc.vector.tensor_copy(
                out=g2[:].rearrange("p (mu ol oh x) -> p mu ol oh x", mu=8, ol=4, oh=4, x=16),
                in_=gt[:, j, :].rearrange("p (oh ol mu x) -> p mu ol oh x", oh=4, ol=4, mu=8, x=16),
            )
            g2s[i] = g2

        def transposes(i):
            g2w = g2s[i][:].bitcast(F32)
            banks = []
            for b in range(2):
                xt = pst.tile([P, 4, P], F32, name="xt", tag="xt")
                for mu in range(4):
                    col = (b * 4 + mu) * P
                    nc.tensor.transpose(xt[:, mu, :], g2w[:, col : col + P], ident[:])
                banks.append(xt)
            xts[i] = banks

        def copy_out(i):
            gr = work.tile([P, FEAT], BF16, name="gr", tag="gr", align_bytes=64)
            grw = gr[:].bitcast(F32)
            for b in range(2):
                dst = grw[:, b * 512 : (b + 1) * 512].rearrange("p (m t u) -> p m t u", m=2, t=P, u=2)
                src = xts[i][b][:].rearrange("p (m u) t -> p m t u", m=2, u=2)
                if i < HEAD_TILES:
                    nc.scalar.copy(out=dst, in_=src)
                else:
                    nc.vector.tensor_copy(out=dst, in_=src)
            grs[i] = gr

        def quantise(i):
            cd = quant.tile([P, 512], U32, name="cd", tag="cd", align_bytes=64)
            sc = quant.tile([P, 512], U8, name="sc", tag="sc", align_bytes=64)
            nc.vector.quantize_mx(out=cd[:].bitcast(E5), scales=sc[:], in_=grs[i][:])
            cds[i] = (cd, sc)

        def multiply(i):
            cd, sc = cds[i]
            first, r = store_of[i]
            j = i - first
            if j == 0:
                osb[first] = outp.tile([P, r, FEAT], F32, name="ot", tag="ot", align_bytes=256)
            ot = osb[first]
            oview = ot[:, j, :].rearrange("p (c m k) -> p c m k", c=32, m=4, k=16)
            for m in range(4):
                acc = pso.tile([P, 512], F32, name="acc", tag="acc")
                nc.tensor.matmul_mx(
                    out=acc[:],
                    lhsT=cd[:, m * P : (m + 1) * P].bitcast(E5),
                    lhsT_scale=sc[:, m * P : (m + 1) * P],
                    rhs=wcodes[:].bitcast(E4),
                    rhs_scale=wsc[:],
                    start=True,
                    stop=True,
                )
                if m >= 2 and i >= NT - TAIL_TILES:
                    nc.vector.tensor_copy(out=oview[:, :, m, :], in_=acc[:].rearrange("p (c k) -> p c k", c=32))
                else:
                    nc.scalar.copy(out=oview[:, :, m, :], in_=acc[:].rearrange("p (c k) -> p c k", c=32))
            if j == r - 1:
                nc.sync.dma_start(out=ov[:, first : first + r, :], in_=ot[:])

        with tc.manual_schedule():
            weight_permute()
            for gt, i0, r in late_loads:
                nc.scalar.dma_start(out=gt[:], in_=gv[:, i0 : i0 + r, :])
            regroup(0)
            weight_transpose(0)
            transposes(0)
            weight_transpose(1)
            regroup(1)
            copy_out(0)
            transposes(1)
            weight_interleave()
            copy_out(1)
            weight_quantise()
            quantise(0)
            quantise(1)
            regroup(2)
            for i in range(NT):
                if 2 <= i + 1 < NT:
                    copy_out(i + 1)
                if i + 3 < NT:
                    regroup(i + 3)
                if 2 <= i + 1 < NT:
                    quantise(i + 1)
                multiply(i)
                if i + 2 < NT:
                    transposes(i + 2)
